import numpy as np
import ml_dtypes


def mxq(x, axis, fmt="e4m3"):
    dtype, down = {"e4m3": (ml_dtypes.float8_e4m3fn, 7), "e5m2": (ml_dtypes.float8_e5m2, 14)}[fmt]
    v = np.moveaxis(np.asarray(x, np.float32).astype(ml_dtypes.bfloat16).astype(np.float64), axis, -1)
    blocks = v.reshape(v.shape[:-1] + (-1, 32))
    amax = np.abs(blocks).max(-1, keepdims=True)
    byte = np.maximum(np.where(amax > 0, np.frexp(amax)[1] - 1 + 127, 0) - down, 1)
    scale = np.exp2(byte - 127.0)
    codes = (blocks / scale).astype(np.float32).astype(dtype).astype(np.float64)
    return np.moveaxis((codes * scale).reshape(v.shape), -1, axis)


WIDE = False


def mx_kscale(k):
    if not WIDE:
        return np.ones(k)
    levels = np.array([10, -10, 5, -5, 0])
    a = np.random.permutation(np.resize(levels, k // 512 * 4)).reshape(k // 512, 4)
    idx = np.arange(k)
    return np.exp2(a[idx // 512, idx % 128 // 32])


BF16 = ml_dtypes.bfloat16


def bf(x):
    return np.asarray(x, np.float32).astype(BF16)


def f64(x):
    return np.asarray(x).astype(np.float64)


B, N, C, R, CO, L = 2, 512, 512, 128, 512, 2
C3 = 3 * C
EPS = 1e-5
LOGIT_STD = 2.5
X_STD = 1.5


def setup_inputs():
    t = mx_kscale(C3)
    th, tx = t[:C], t[C:C + C]
    tw = np.concatenate([th, tx, tx])
    e = np.exp(np.maximum(np.random.standard_normal((N, N)) * LOGIT_STD, 0.0))
    return {"h": bf(np.random.standard_normal((B, C, N)) * X_STD * th[None, :, None]),
            "x1": bf(np.random.standard_normal((B, C, N)) * 0.4 * tx[None, :, None]),
            "adp": bf(e / e.sum(1, keepdims=True)),
            "wg": bf(np.random.standard_normal((C, C3)) / np.sqrt(C) / tw[None, :]),
            "bg": bf(np.random.standard_normal(C) * 0.2),
            "gamma": bf(1.0 + 0.1 * np.random.standard_normal(C)),
            "beta": bf(np.random.standard_normal(C) * 0.2),
            "rmean": bf(np.random.standard_normal(C) * 0.2),
            "rvar": bf(np.random.uniform(0.5, 1.5, C))}


def reference(h, x1, adp, wg, bg, gamma, beta, rmean, rvar):
    h, x1 = f64(h), f64(x1)
    x2 = (mxq(x1.reshape(B * C, N), 1, "e4m3") @ mxq(f64(adp), 1, "e4m3").T).reshape(B, C, N)
    cat = np.concatenate([h, x1, x2], axis=1)
    g = (mxq(f64(wg), 1, "e4m3") @ mxq(cat, 1, "e4m3")) + f64(bg)[None, :, None]
    inv = f64(gamma) / np.sqrt(f64(rvar) + EPS)
    return g * inv[None, :, None] + (f64(beta) - f64(rmean) * inv)[None, :, None]

@@ -1,0 +1,237 @@
+from contextlib import ExitStack
+
+import concourse.mybir as mybir
+from concourse.masks import make_identity
+
+F32 = mybir.dt.float32
+BF16 = mybir.dt.bfloat16
+U32 = mybir.dt.uint32
+U8 = mybir.dt.uint8
+FP8X4 = mybir.dt.float8_e4m3fn_x4
+ACT = mybir.ActivationFunctionType
+ALU = mybir.AluOpType
+
+P = 128
+PACK = 4
+K_PASS = P * PACK
+BATCH = 2
+CH = 512
+NODES = 512
+GROUPS = 3
+TILES = 4
+BANK = 512
+EPS = 1e-5
+
+FLOPS = 2 * BATCH * CH * NODES * NODES + 2 * BATCH * CH * GROUPS * CH * NODES
+
+
+def tile_spatialgcn_pb_kernel(tc, h, x1, adp, wg, bg, gamma, beta, rmean, rvar, out):
+    nc = tc.nc
+    with ExitStack() as ctx:
+        const = ctx.enter_context(tc.tile_pool(name="const", bufs=1))
+        rows = ctx.enter_context(tc.tile_pool(name="rows", bufs=1))
+        grouped = ctx.enter_context(tc.tile_pool(name="grouped", bufs=1))
+        mx = ctx.enter_context(tc.tile_pool(name="mx", bufs=1))
+        results = ctx.enter_context(tc.tile_pool(name="results", bufs=1))
+        psum = ctx.enter_context(tc.psum_pool(name="psum", bufs=8))
+        ctx.enter_context(tc.manual_schedule())
+
+        def load_channels_first(name, src):
+            tile_ = rows.tile([P, PACK * NODES], BF16, name=name)
+            nc.sync.dma_start(
+                out=tile_[:].rearrange("p (u r) -> p u r", u=2),
+                in_=src.rearrange("(u q e) n -> q u (e n)", u=2, e=2),
+            )
+            return tile_
+
+        def load_channel_vector(name, vec):
+            tile_ = const.tile([P, TILES], BF16, name=name)
+            nc.scalar.dma_start(out=tile_[:], in_=vec.rearrange("(p t) -> p t", t=TILES))
+            return tile_
+
+        rvar_sb = load_channel_vector("rvar_sb", rvar)
+        gamma_sb = load_channel_vector("gamma_sb", gamma)
+        bg_sb = load_channel_vector("bg_sb", bg)
+        rmean_sb = load_channel_vector("rmean_sb", rmean)
+        beta_sb = load_channel_vector("beta_sb", beta)
+
+        x1_rows = [None, None]
+        h_rows = [None, None]
+        x1_rows[0] = load_channels_first("x1_rows0", x1[0])
+        adp_rows = rows.tile([P, TILES * NODES], BF16, name="adp_rows")
+        nc.sync.dma_start(
+            out=adp_rows[:].rearrange("p (j v) -> p j v", j=TILES),
+            in_=adp.rearrange("(j p) v -> p j v", p=P),
+        )
+        x1_rows[1] = load_channels_first("x1_rows1", x1[1])
+        wg_rows = []
+        for i in range(2):
+            wg_half = rows.tile([P, 2 * GROUPS * CH], BF16, name="wg_rows%d" % i)
+            nc.sync.dma_start(
+                out=wg_half[:].rearrange("p (r c) -> p r c", r=2),
+                in_=wg.rearrange("(p t) c -> p t c", t=TILES)[:, 2 * i : 2 * i + 2, :],
+            )
+            wg_rows.append(wg_half)
+        h_rows[0] = load_channels_first("h_rows0", h[0])
+        h_rows[1] = load_channels_first("h_rows1", h[1])
+
+        ident = const.tile([P, P], F32, name="ident")
+        make_identity(nc, ident[:])
+
+        def new_operand(name, cols):
+            values = grouped.tile([P, cols * PACK], BF16, name=name + "_values", align_bytes=64)
+            codes = mx.tile([P, cols], U32, name=name + "_codes", align_bytes=64)
+            scales = mx.tile([P, cols], U8, name=name + "_scales", align_bytes=64)
+            return {"values": values, "codes": codes, "scales": scales}
+
+        def quantise(operand):
+            nc.vector.quantize_mx(
+                out=operand["codes"][:].bitcast(FP8X4),
+                scales=operand["scales"][:],
+                in_=operand["values"][:],
+            )
+
+        def transpose_256_rows(src_words, operand, first_col):
+            bank = psum.tile([P, BANK], F32, tag="bank", name="t_bank")
+            for u in range(2):
+                for r in range(2):
+                    nc.tensor.transpose(
+                        bank[:, (2 * u + r) * P : (2 * u + r + 1) * P],
+                        src_words[:, r, u * P : (u + 1) * P],
+                        ident[:],
+                    )
+            words = operand["values"][:].bitcast(F32)
+            nc.scalar.copy(
+                out=words[:, 2 * first_col : 2 * first_col + BANK].rearrange("p (c u) -> p c u", u=2),
+                in_=bank[:].rearrange("p (u c) -> p c u", u=2),
+            )
+
+        def transpose_512_rows(rows_tile, operand):
+            src_words = rows_tile[:].bitcast(F32).rearrange("p (t m) -> p t m", t=TILES)
+            for i in range(2):
+                transpose_256_rows(src_words[:, 2 * i : 2 * i + 2, :], operand, 256 * i)
+
+        def regroup(rows_tile, operand):
+            nc.vector.tensor_copy(
+                out=operand["values"][:].rearrange("p (c i t) -> p c t i", i=4, t=PACK),
+                in_=rows_tile[:].rearrange("p (t c i) -> p c t i", t=PACK, i=4),
+            )
+
+        def hop(b):
+            for j in range(TILES):
+                bank = psum.tile([P, BANK], F32, tag="bank", name="x2_bank")
+                for t in range(TILES):
+                    nc.tensor.matmul_mx(
+                        out=bank[:, t * P : (t + 1) * P],
+                        lhsT=x1T[b]["codes"][:, t * P : (t + 1) * P].bitcast(FP8X4),
+                        lhsT_scale=x1T[b]["scales"][:, t * P : (t + 1) * P],
+                        rhs=adpT["codes"][:, j * P : (j + 1) * P].bitcast(FP8X4),
+                        rhs_scale=adpT["scales"][:, j * P : (j + 1) * P],
+                        start=True,
+                        stop=True,
+                    )
+                nc.scalar.copy(
+                    out=cat[b][2]["values"][:, j * BANK : (j + 1) * BANK].rearrange("p (w t) -> p w t", t=PACK),
+                    in_=bank[:].rearrange("p (t w) -> p w t", t=PACK),
+                )
+
+        acc = {}
+
+        def conv(b, g, first, last):
+            for ot in range(TILES):
+                if first:
+                    acc[(b, ot)] = psum.tile([P, BANK], F32, tag="bank", name="acc")
+                weights = wgT[ot // 2][g]
+                cols = slice((ot % 2) * P, (ot % 2 + 1) * P)
+                nc.tensor.matmul_mx(
+                    out=acc[(b, ot)][:],
+                    lhsT=weights["codes"][:, cols].bitcast(FP8X4),
+                    lhsT_scale=weights["scales"][:, cols],
+                    rhs=cat[b][g]["codes"][:].bitcast(FP8X4),
+                    rhs_scale=cat[b][g]["scales"][:],
+                    start=first,
+                    stop=last,
+                )
+
+        def finish(b):
+            out_rows = out[b].rearrange("(p t) n -> p t n", t=TILES)
+            for i in range(2):
+                result = results.tile([P, 2 * NODES], F32, name="result%d%d" % (b, i))
+                nc.scalar.activation(
+                    out=result[:, 0:NODES],
+                    in_=acc[(b, 2 * i)][:],
+                    func=ACT.Identity,
+                    scale=inv[:, 2 * i : 2 * i + 1],
+                    bias=shift[:, 2 * i : 2 * i + 1],
+                )
+                nc.vector.tensor_scalar(
+                    out=result[:, NODES : 2 * NODES],
+                    in0=acc[(b, 2 * i + 1)][:],
+                    scalar1=inv[:, 2 * i + 1 : 2 * i + 2],
+                    scalar2=shift[:, 2 * i + 1 : 2 * i + 2],
+                    op0=ALU.mult,
+                    op1=ALU.add,
+                )
+                nc.sync.dma_start(
+                    out=out_rows[:, 2 * i : 2 * i + 2, :],
+                    in_=result[:].rearrange("p (r n) -> p r n", r=2),
+                )
+
+        x1T = [new_operand("x1T%d" % b, CH) for b in range(BATCH)]
+        adpT = new_operand("adpT", NODES)
+        wgT = [[new_operand("wgT%d%d" % (i, g), 2 * P) for g in range(GROUPS)] for i in range(2)]
+        cat = [[new_operand("cat%d%d" % (b, g), NODES) for g in range(GROUPS)] for b in range(BATCH)]
+
+        var_eps = const.tile([P, TILES], F32, name="var_eps")
+        std = const.tile([P, TILES], F32, name="std")
+        rstd = const.tile([P, TILES], F32, name="rstd")
+        inv = const.tile([P, TILES], F32, name="inv")
+        centred = const.tile([P, TILES], F32, name="centred")
+        scaled = const.tile([P, TILES], F32, name="scaled")
+        shift = const.tile([P, TILES], F32, name="shift")
+        nc.vector.tensor_scalar_add(out=var_eps[:], in0=rvar_sb[:], scalar1=EPS)
+        nc.scalar.sqrt(out=std[:], in_=var_eps[:])
+        nc.vector.tensor_sub(out=centred[:], in0=bg_sb[:], in1=rmean_sb[:])
+
+        regroup(x1_rows[0], cat[0][1])
+        transpose_512_rows(x1_rows[0], x1T[0])
+        transpose_512_rows(adp_rows, adpT)
+
+        nc.vector.reciprocal(out=rstd[:], in_=std[:])
+        nc.vector.tensor_mul(out=inv[:], in0=gamma_sb[:], in1=rstd[:])
+        nc.vector.tensor_mul(out=scaled[:], in0=centred[:], in1=inv[:])
+        nc.vector.tensor_add(out=shift[:], in0=scaled[:], in1=beta_sb[:])
+
+        quantise(cat[0][1])
+        quantise(x1T[0])
+        quantise(adpT)
+        transpose_512_rows(x1_rows[1], x1T[1])
+        regroup(x1_rows[1], cat[1][1])
+        hop(0)
+        quantise(x1T[1])
+        quantise(cat[1][1])
+        for g in range(GROUPS):
+            wg_words = wg_rows[0][:].bitcast(F32).rearrange("p (r m) -> p r m", r=2)
+            transpose_256_rows(wg_words[:, :, 256 * g : 256 * (g + 1)], wgT[0][g], 0)
+        quantise(cat[0][2])
+        hop(1)
+        for g in range(GROUPS):
+            quantise(wgT[0][g])
+        regroup(h_rows[0], cat[0][0])
+        for g in range(GROUPS):
+            wg_words = wg_rows[1][:].bitcast(F32).rearrange("p (r m) -> p r m", r=2)
+            transpose_256_rows(wg_words[:, :, 256 * g : 256 * (g + 1)], wgT[1][g], 0)
+        quantise(cat[0][0])
+        quantise(cat[1][2])
+        for g in range(GROUPS):
+            quantise(wgT[1][g])
+        regroup(h_rows[1], cat[1][0])
+        conv(0, 1, True, False)
+        conv(0, 2, False, False)
+        conv(0, 0, False, True)
+        quantise(cat[1][0])
+        conv(1, 1, True, False)
+        conv(1, 2, False, False)
+        finish(0)
+        conv(1, 0, False, True)
+        finish(1)

@@ -21,6 +21,7 @@ GROUPS = 3
 TILES = 4
 BANK = 512
 EPS = 1e-5
+CONV_ORDER = (1, 0, 2)
 
 FLOPS = 2 * BATCH * CH * NODES * NODES + 2 * BATCH * CH * GROUPS * CH * NODES
 
@@ -135,47 +136,50 @@ def tile_spatialgcn_pb_kernel(tc, h, x1, adp, wg, bg, gamma, beta, rmean, rvar, 
                     in_=bank[:].rearrange("p (t w) -> p w t", t=PACK),
                 )
 
-        acc = {}
-
-        def conv(b, g, first, last):
-            for ot in range(TILES):
-                if first:
-                    acc[(b, ot)] = psum.tile([P, BANK], F32, tag="bank", name="acc")
-                weights = wgT[ot // 2][g]
-                cols = slice((ot % 2) * P, (ot % 2 + 1) * P)
-                nc.tensor.matmul_mx(
-                    out=acc[(b, ot)][:],
-                    lhsT=weights["codes"][:, cols].bitcast(FP8X4),
-                    lhsT_scale=weights["scales"][:, cols],
-                    rhs=cat[b][g]["codes"][:].bitcast(FP8X4),
-                    rhs_scale=cat[b][g]["scales"][:],
-                    start=first,
-                    stop=last,
-                )
-
-        def finish(b):
+        def conv(b):
             out_rows = out[b].rearrange("(p t) n -> p t n", t=TILES)
-            for i in range(2):
-                result = results.tile([P, 2 * NODES], F32, name="result%d%d" % (b, i))
-                nc.scalar.activation(
-                    out=result[:, 0:NODES],
-                    in_=acc[(b, 2 * i)][:],
-                    func=ACT.Identity,
-                    scale=inv[:, 2 * i : 2 * i + 1],
-                    bias=shift[:, 2 * i : 2 * i + 1],
-                )
-                nc.vector.tensor_scalar(
-                    out=result[:, NODES : 2 * NODES],
-                    in0=acc[(b, 2 * i + 1)][:],
-                    scalar1=inv[:, 2 * i + 1 : 2 * i + 2],
-                    scalar2=shift[:, 2 * i + 1 : 2 * i + 2],
-                    op0=ALU.mult,
-                    op1=ALU.add,
-                )
-                nc.sync.dma_start(
-                    out=out_rows[:, 2 * i : 2 * i + 2, :],
-                    in_=result[:].rearrange("p (r n) -> p r n", r=2),
-                )
+            for ot in range(TILES):
+                acc = psum.tile([P, BANK], F32, tag="bank", name="acc")
+                cols = slice((ot % 2) * P, (ot % 2 + 1) * P)
+                for g in CONV_ORDER:
+                    weights = wgT[ot // 2][g]
+                    nc.tensor.matmul_mx(
+                        out=acc[:],
+                        lhsT=weights["codes"][:, cols].bitcast(FP8X4),
+                        lhsT_scale=weights["scales"][:, cols],
+                        rhs=cat[b][g]["codes"][:].bitcast(FP8X4),
+                        rhs_scale=cat[b][g]["scales"][:],
+                        start=(g == CONV_ORDER[0]),
+                        stop=(g == CONV_ORDER[-1]),
+                    )
+                result = results.tile([P, NODES], F32, name="result%d%d" % (b, ot))
+                if ot % 2 == 0:
+                    nc.scalar.activation(
+                        out=result[:],
+                        in_=acc[:],
+                        func=ACT.Identity,
+                        scale=inv[:, ot : ot + 1],
+                        bias=shift[:, ot : ot + 1],
+                    )
+                else:
+                    nc.vector.tensor_scalar(
+                        out=result[:],
+                        in0=acc[:],
+                        scalar1=inv[:, ot : ot + 1],
+                        scalar2=shift[:, ot : ot + 1],
+                        op0=ALU.mult,
+                        op1=ALU.add,
+                    )
+                nc.sync.dma_start(out=out_rows[:, ot, :], in_=result[:])
+
+        def transpose_wg_half(i):
+            wg_words = wg_rows[i][:].bitcast(F32).rearrange("p (r m) -> p r m", r=2)
+            for g in range(GROUPS):
+                transpose_256_rows(wg_words[:, :, 256 * g : 256 * (g + 1)], wgT[i][g], 0)
+
+        def quantise_wg_half(i):
+            for g in range(GROUPS):
+                quantise(wgT[i][g])
 
         x1T = [new_operand("x1T%d" % b, CH) for b in range(BATCH)]
         adpT = new_operand("adpT", NODES)
@@ -195,7 +199,6 @@ def tile_spatialgcn_pb_kernel(tc, h, x1, adp, wg, bg, gamma, beta, rmean, rvar, 
 
         regroup(x1_rows[0], cat[0][1])
         transpose_512_rows(x1_rows[0], x1T[0])
-        transpose_512_rows(adp_rows, adpT)
 
         nc.vector.reciprocal(out=rstd[:], in_=std[:])
         nc.vector.tensor_mul(out=inv[:], in0=gamma_sb[:], in1=rstd[:])
@@ -204,34 +207,23 @@ def tile_spatialgcn_pb_kernel(tc, h, x1, adp, wg, bg, gamma, beta, rmean, rvar, 
 
         quantise(cat[0][1])
         quantise(x1T[0])
+        transpose_512_rows(adp_rows, adpT)
+        regroup(x1_rows[1], cat[1][1])
         quantise(adpT)
         transpose_512_rows(x1_rows[1], x1T[1])
-        regroup(x1_rows[1], cat[1][1])
-        hop(0)
         quantise(x1T[1])
         quantise(cat[1][1])
-        for g in range(GROUPS):
-            wg_words = wg_rows[0][:].bitcast(F32).rearrange("p (r m) -> p r m", r=2)
-            transpose_256_rows(wg_words[:, :, 256 * g : 256 * (g + 1)], wgT[0][g], 0)
-        quantise(cat[0][2])
-        hop(1)
-        for g in range(GROUPS):
-            quantise(wgT[0][g])
+        transpose_wg_half(0)
+        quantise_wg_half(0)
+        hop(0)
+        transpose_wg_half(1)
         regroup(h_rows[0], cat[0][0])
-        for g in range(GROUPS):
-            wg_words = wg_rows[1][:].bitcast(F32).rearrange("p (r m) -> p r m", r=2)
-            transpose_256_rows(wg_words[:, :, 256 * g : 256 * (g + 1)], wgT[1][g], 0)
+        quantise(cat[0][2])
         quantise(cat[0][0])
-        quantise(cat[1][2])
-        for g in range(GROUPS):
-            quantise(wgT[1][g])
+        quantise_wg_half(1)
+        hop(1)
         regroup(h_rows[1], cat[1][0])
-        conv(0, 1, True, False)
-        conv(0, 2, False, False)
-        conv(0, 0, False, True)
         quantise(cat[1][0])
-        conv(1, 1, True, False)
-        conv(1, 2, False, False)
-        finish(0)
-        conv(1, 0, False, True)
-        finish(1)
+        quantise(cat[1][2])
+        conv(0)
+        conv(1)

@@ -20,6 +20,7 @@ NODES = 512
 GROUPS = 3
 TILES = 4
 BANK = 512
+PIECE = 2 * BANK
 EPS = 1e-5
 CONV_ORDER = (1, 0, 2)
 
@@ -45,16 +46,21 @@ def tile_spatialgcn_pb_kernel(tc, h, x1, adp, wg, bg, gamma, beta, rmean, rvar, 
             )
             return tile_
 
-        def load_channel_vector(name, vec):
+        def load_channel_vector(queue, name, vec):
             tile_ = const.tile([P, TILES], BF16, name=name)
-            nc.scalar.dma_start(out=tile_[:], in_=vec.rearrange("(p t) -> p t", t=TILES))
+            queue.dma_start(out=tile_[:], in_=vec.rearrange("(p t) -> p t", t=TILES))
             return tile_
 
-        rvar_sb = load_channel_vector("rvar_sb", rvar)
-        gamma_sb = load_channel_vector("gamma_sb", gamma)
-        bg_sb = load_channel_vector("bg_sb", bg)
-        rmean_sb = load_channel_vector("rmean_sb", rmean)
-        beta_sb = load_channel_vector("beta_sb", beta)
+        def load_wg_half(i):
+            pieces = []
+            for m in range(GROUPS):
+                piece = rows.tile([P, PIECE], BF16, name="wg_rows%d%d" % (i, m))
+                first = (GROUPS * i + m) * PIECE
+                nc.sync.dma_start(out=piece[:], in_=wg_flat[:, first : first + PIECE])
+                pieces.append(piece)
+            return pieces
+
+        rvar_sb = load_channel_vector(nc.scalar, "rvar_sb", rvar)
 
         x1_rows = [None, None]
         h_rows = [None, None]
@@ -65,16 +71,16 @@ def tile_spatialgcn_pb_kernel(tc, h, x1, adp, wg, bg, gamma, beta, rmean, rvar, 
             in_=adp.rearrange("(j p) v -> p j v", p=P),
         )
         x1_rows[1] = load_channels_first("x1_rows1", x1[1])
-        wg_rows = []
-        for i in range(2):
-            wg_half = rows.tile([P, 2 * GROUPS * CH], BF16, name="wg_rows%d" % i)
-            nc.sync.dma_start(
-                out=wg_half[:].rearrange("p (r c) -> p r c", r=2),
-                in_=wg.rearrange("(p t) c -> p t c", t=TILES)[:, 2 * i : 2 * i + 2, :],
-            )
-            wg_rows.append(wg_half)
+        wg_flat = wg.rearrange("(p t) c -> p (t c)", t=TILES)
+        wg_rows = [None, None]
+        wg_rows[0] = load_wg_half(0)
         h_rows[0] = load_channels_first("h_rows0", h[0])
+        wg_rows[1] = load_wg_half(1)
         h_rows[1] = load_channels_first("h_rows1", h[1])
+        gamma_sb = load_channel_vector(nc.sync, "gamma_sb", gamma)
+        bg_sb = load_channel_vector(nc.sync, "bg_sb", bg)
+        rmean_sb = load_channel_vector(nc.sync, "rmean_sb", rmean)
+        beta_sb = load_channel_vector(nc.sync, "beta_sb", beta)
 
         ident = const.tile([P, P], F32, name="ident")
         make_identity(nc, ident[:])
@@ -140,9 +146,10 @@ def tile_spatialgcn_pb_kernel(tc, h, x1, adp, wg, bg, gamma, beta, rmean, rvar, 
             out_rows = out[b].rearrange("(p t) n -> p t n", t=TILES)
             for ot in range(TILES):
                 acc = psum.tile([P, BANK], F32, tag="bank", name="acc")
-                cols = slice((ot % 2) * P, (ot % 2 + 1) * P)
                 for g in CONV_ORDER:
-                    weights = wgT[ot // 2][g]
+                    unit = GROUPS * (ot % 2) + g
+                    weights = wgT[ot // 2][unit // 2]
+                    cols = slice((unit % 2) * P, (unit % 2 + 1) * P)
                     nc.tensor.matmul_mx(
                         out=acc[:],
                         lhsT=weights["codes"][:, cols].bitcast(FP8X4),
@@ -173,17 +180,17 @@ def tile_spatialgcn_pb_kernel(tc, h, x1, adp, wg, bg, gamma, beta, rmean, rvar, 
                 nc.sync.dma_start(out=out_rows[:, ot, :], in_=result[:])
 
         def transpose_wg_half(i):
-            wg_words = wg_rows[i][:].bitcast(F32).rearrange("p (r m) -> p r m", r=2)
-            for g in range(GROUPS):
-                transpose_256_rows(wg_words[:, :, 256 * g : 256 * (g + 1)], wgT[i][g], 0)
+            for m in range(GROUPS):
+                unit_words = wg_rows[i][m][:].bitcast(F32).rearrange("p (k w) -> p k w", k=2)
+                transpose_256_rows(unit_words, wgT[i][m], 0)
 
         def quantise_wg_half(i):
-            for g in range(GROUPS):
-                quantise(wgT[i][g])
+            for m in range(GROUPS):
+                quantise(wgT[i][m])
 
         x1T = [new_operand("x1T%d" % b, CH) for b in range(BATCH)]
         adpT = new_operand("adpT", NODES)
-        wgT = [[new_operand("wgT%d%d" % (i, g), 2 * P) for g in range(GROUPS)] for i in range(2)]
+        wgT = [[new_operand("wgT%d%d" % (i, m), 2 * P) for m in range(GROUPS)] for i in range(2)]
         cat = [[new_operand("cat%d%d" % (b, g), NODES) for g in range(GROUPS)] for b in range(BATCH)]
 
         var_eps = const.tile([P, TILES], F32, name="var_eps")
@@ -195,16 +202,11 @@ def tile_spatialgcn_pb_kernel(tc, h, x1, adp, wg, bg, gamma, beta, rmean, rvar, 
         shift = const.tile([P, TILES], F32, name="shift")
         nc.vector.tensor_scalar_add(out=var_eps[:], in0=rvar_sb[:], scalar1=EPS)
         nc.scalar.sqrt(out=std[:], in_=var_eps[:])
-        nc.vector.tensor_sub(out=centred[:], in0=bg_sb[:], in1=rmean_sb[:])
 
         regroup(x1_rows[0], cat[0][1])
         transpose_512_rows(x1_rows[0], x1T[0])
 
         nc.vector.reciprocal(out=rstd[:], in_=std[:])
-        nc.vector.tensor_mul(out=inv[:], in0=gamma_sb[:], in1=rstd[:])
-        nc.vector.tensor_mul(out=scaled[:], in0=centred[:], in1=inv[:])
-        nc.vector.tensor_add(out=shift[:], in0=scaled[:], in1=beta_sb[:])
-
         quantise(cat[0][1])
         quantise(x1T[0])
         transpose_512_rows(adp_rows, adpT)
@@ -223,6 +225,10 @@ def tile_spatialgcn_pb_kernel(tc, h, x1, adp, wg, bg, gamma, beta, rmean, rvar, 
         quantise_wg_half(1)
         hop(1)
         regroup(h_rows[1], cat[1][0])
+        nc.vector.tensor_mul(out=inv[:], in0=gamma_sb[:], in1=rstd[:])
+        nc.vector.tensor_sub(out=centred[:], in0=bg_sb[:], in1=rmean_sb[:])
+        nc.vector.tensor_mul(out=scaled[:], in0=centred[:], in1=inv[:])
+        nc.vector.tensor_add(out=shift[:], in0=scaled[:], in1=beta_sb[:])
         quantise(cat[1][0])
         quantise(cat[1][2])
         conv(0)

@@ -62,6 +62,14 @@ def tile_spatialgcn_pb_kernel(tc, h, x1, adp, wg, bg, gamma, beta, rmean, rvar, 
 
         rvar_sb = load_channel_vector(nc.scalar, "rvar_sb", rvar)
 
+        zeros = const.tile([P, BANK], BF16, name="zeros")
+        nc.vector.memset(zeros[:], 0.0)
+
+        def keep_warm(count):
+            bank = psum.tile([P, BANK], F32, tag="bank", name="warm_bank")
+            for i in range(count):
+                nc.tensor.matmul(bank[:], lhsT=zeros[:, 0:P], rhs=zeros[:], start=True, stop=True)
+
         x1_rows = [None, None]
         h_rows = [None, None]
         x1_rows[0] = load_channels_first("x1_rows0", x1[0])
@@ -203,16 +211,20 @@ def tile_spatialgcn_pb_kernel(tc, h, x1, adp, wg, bg, gamma, beta, rmean, rvar, 
         nc.vector.tensor_scalar_add(out=var_eps[:], in0=rvar_sb[:], scalar1=EPS)
         nc.scalar.sqrt(out=std[:], in_=var_eps[:])
 
+        keep_warm(5)
         regroup(x1_rows[0], cat[0][1])
         transpose_512_rows(x1_rows[0], x1T[0])
+        keep_warm(2)
 
         nc.vector.reciprocal(out=rstd[:], in_=std[:])
         quantise(cat[0][1])
         quantise(x1T[0])
         transpose_512_rows(adp_rows, adpT)
+        keep_warm(2)
         regroup(x1_rows[1], cat[1][1])
         quantise(adpT)
         transpose_512_rows(x1_rows[1], x1T[1])
+        keep_warm(2)
         quantise(x1T[1])
         quantise(cat[1][1])
         transpose_wg_half(0)

@@ -22,7 +22,7 @@ TILES = 4
 BANK = 512
 PIECE = 2 * BANK
 EPS = 1e-5
-CONV_ORDER = (1, 0, 2)
+CONV_ORDER = (1, 2, 0)
 
 FLOPS = 2 * BATCH * CH * NODES * NODES + 2 * BATCH * CH * GROUPS * CH * NODES
 
@@ -151,27 +151,27 @@ def tile_spatialgcn_pb_kernel(tc, h, x1, adp, wg, bg, gamma, beta, rmean, rvar, 
                 )
 
         def conv(b):
-            out_rows = out[b].rearrange("(p t) n -> p t n", t=TILES)
-            for ot in range(TILES):
-                acc = psum.tile([P, BANK], F32, tag="bank", name="acc")
-                for g in CONV_ORDER:
-                    unit = GROUPS * (ot % 2) + g
-                    weights = wgT[ot // 2][unit // 2]
-                    cols = slice((unit % 2) * P, (unit % 2 + 1) * P)
-                    nc.tensor.matmul_mx(
-                        out=acc[:],
-                        lhsT=weights["codes"][:, cols].bitcast(FP8X4),
-                        lhsT_scale=weights["scales"][:, cols],
-                        rhs=cat[b][g]["codes"][:].bitcast(FP8X4),
-                        rhs_scale=cat[b][g]["scales"][:],
-                        start=(g == CONV_ORDER[0]),
-                        stop=(g == CONV_ORDER[-1]),
-                    )
-                result = results.tile([P, NODES], F32, name="result%d%d" % (b, ot))
-                if ot % 2 == 0:
+            def conv_pass(acc, ot, g, nodes):
+                unit = GROUPS * (ot % 2) + g
+                weights = wgT[ot // 2][unit // 2]
+                cols = slice((unit % 2) * P, (unit % 2 + 1) * P)
+                nc.tensor.matmul_mx(
+                    out=acc[:, 0 : nodes.stop - nodes.start],
+                    lhsT=weights["codes"][:, cols].bitcast(FP8X4),
+                    lhsT_scale=weights["scales"][:, cols],
+                    rhs=cat[b][g]["codes"][:, nodes].bitcast(FP8X4),
+                    rhs_scale=cat[b][g]["scales"][:, nodes],
+                    start=(g == CONV_ORDER[0]),
+                    stop=(g == CONV_ORDER[-1]),
+                )
+
+            def leave(acc, ot, nodes, on_scalar):
+                width = nodes.stop - nodes.start
+                result = results.tile([P, width], F32, name="result%d%d%d" % (b, ot, nodes.start))
+                if on_scalar:
                     nc.scalar.activation(
                         out=result[:],
-                        in_=acc[:],
+                        in_=acc[:, 0:width],
                         func=ACT.Identity,
                         scale=inv[:, ot : ot + 1],
                         bias=shift[:, ot : ot + 1],
@@ -179,13 +179,35 @@ def tile_spatialgcn_pb_kernel(tc, h, x1, adp, wg, bg, gamma, beta, rmean, rvar, 
                 else:
                     nc.vector.tensor_scalar(
                         out=result[:],
-                        in0=acc[:],
+                        in0=acc[:, 0:width],
                         scalar1=inv[:, ot : ot + 1],
                         scalar2=shift[:, ot : ot + 1],
                         op0=ALU.mult,
                         op1=ALU.add,
                     )
-                nc.sync.dma_start(out=out_rows[:, ot, :], in_=result[:])
+                nc.sync.dma_start(out=out_rows[:, ot, nodes], in_=result[:])
+
+            out_rows = out[b].rearrange("(p t) n -> p t n", t=TILES)
+            everything = slice(0, NODES)
+            if b == 0:
+                groups = [[(0, everything), (1, everything)], [(2, everything)], [(3, everything)]]
+            else:
+                groups = [[(0, everything), (1, everything), (2, everything), (3, slice(0, 256)), (3, slice(256, 512))]]
+            for group in groups:
+                banks = []
+                for ot, nodes in group:
+                    acc = psum.tile([P, BANK], F32, tag="bank", name="acc")
+                    banks.append(acc)
+                    conv_pass(acc, ot, CONV_ORDER[0], nodes)
+                if b == 0:
+                    for g in CONV_ORDER[1:]:
+                        for acc, (ot, nodes) in zip(banks, group):
+                            conv_pass(acc, ot, g, nodes)
+                for acc, (ot, nodes) in zip(banks, group):
+                    if b == 1:
+                        for g in CONV_ORDER[1:]:
+                            conv_pass(acc, ot, g, nodes)
+                    leave(acc, ot, nodes, b == 0 or ot % 2 == 1 and nodes.start == 0)
 
         def transpose_wg_half(i):
             for m in range(GROUPS):
@@ -234,14 +256,16 @@ def tile_spatialgcn_pb_kernel(tc, h, x1, adp, wg, bg, gamma, beta, rmean, rvar, 
         regroup(h_rows[0], cat[0][0])
         quantise(cat[0][2])
         quantise(cat[0][0])
-        quantise_wg_half(1)
-        hop(1)
-        regroup(h_rows[1], cat[1][0])
+        quantise(wgT[1][0])
         nc.vector.tensor_mul(out=inv[:], in0=gamma_sb[:], in1=rstd[:])
         nc.vector.tensor_sub(out=centred[:], in0=bg_sb[:], in1=rmean_sb[:])
+        quantise(wgT[1][1])
         nc.vector.tensor_mul(out=scaled[:], in0=centred[:], in1=inv[:])
+        quantise(wgT[1][2])
+        hop(1)
+        regroup(h_rows[1], cat[1][0])
         nc.vector.tensor_add(out=shift[:], in0=scaled[:], in1=beta_sb[:])
-        quantise(cat[1][0])
         quantise(cat[1][2])
+        quantise(cat[1][0])
         conv(0)
         conv(1)

@@ -62,17 +62,22 @@ def tile_spatialgcn_pb_kernel(tc, h, x1, adp, wg, bg, gamma, beta, rmean, rvar, 
 
         rvar_sb = load_channel_vector(nc.scalar, "rvar_sb", rvar)
 
-        zeros = const.tile([P, BANK], BF16, name="zeros")
+        zeros = const.tile([P, 2 * P], BF16, name="zeros")
         nc.vector.memset(zeros[:], 0.0)
 
         def keep_warm(count):
             bank = psum.tile([P, BANK], F32, tag="bank", name="warm_bank")
             for i in range(count):
-                nc.tensor.matmul(bank[:], lhsT=zeros[:, 0:P], rhs=zeros[:], start=True, stop=True)
+                nc.tensor.matmul(bank[:, 0 : 2 * P], lhsT=zeros[:, 0:P], rhs=zeros[:], start=True, stop=True)
 
         x1_rows = [None, None]
         h_rows = [None, None]
-        x1_rows[0] = load_channels_first("x1_rows0", x1[0])
+        x1_rows[0] = rows.tile([P, PACK * NODES], BF16, name="x1_rows0")
+        for u in range(2):
+            nc.sync.dma_start(
+                out=x1_rows[0][:, u * 2 * NODES : (u + 1) * 2 * NODES],
+                in_=x1[0].rearrange("(u q e) n -> u q (e n)", u=2, e=2)[u],
+            )
         adp_rows = rows.tile([P, TILES * NODES], BF16, name="adp_rows")
         nc.sync.dma_start(
             out=adp_rows[:].rearrange("p (j v) -> p j v", j=TILES),
@@ -233,20 +238,20 @@ def tile_spatialgcn_pb_kernel(tc, h, x1, adp, wg, bg, gamma, beta, rmean, rvar, 
         nc.vector.tensor_scalar_add(out=var_eps[:], in0=rvar_sb[:], scalar1=EPS)
         nc.scalar.sqrt(out=std[:], in_=var_eps[:])
 
-        keep_warm(5)
+        keep_warm(8)
         regroup(x1_rows[0], cat[0][1])
         transpose_512_rows(x1_rows[0], x1T[0])
-        keep_warm(2)
+        keep_warm(4)
 
         nc.vector.reciprocal(out=rstd[:], in_=std[:])
         quantise(cat[0][1])
         quantise(x1T[0])
         transpose_512_rows(adp_rows, adpT)
-        keep_warm(2)
+        keep_warm(4)
         regroup(x1_rows[1], cat[1][1])
         quantise(adpT)
         transpose_512_rows(x1_rows[1], x1T[1])
-        keep_warm(2)
+        keep_warm(4)
         quantise(x1T[1])
         quantise(cat[1][1])
         transpose_wg_half(0)

@@ -22,7 +22,7 @@ TILES = 4
 BANK = 512
 PIECE = 2 * BANK
 EPS = 1e-5
-CONV_ORDER = (1, 2, 0)
+CONV_ORDER = ((1, 2, 0), (1, 0, 2))
 
 FLOPS = 2 * BATCH * CH * NODES * NODES + 2 * BATCH * CH * GROUPS * CH * NODES
 
@@ -35,7 +35,7 @@ def tile_spatialgcn_pb_kernel(tc, h, x1, adp, wg, bg, gamma, beta, rmean, rvar, 
         grouped = ctx.enter_context(tc.tile_pool(name="grouped", bufs=1))
         mx = ctx.enter_context(tc.tile_pool(name="mx", bufs=1))
         results = ctx.enter_context(tc.tile_pool(name="results", bufs=1))
-        psum = ctx.enter_context(tc.psum_pool(name="psum", bufs=8))
+        psum = ctx.enter_context(tc.psum_pool(name="psum", bufs=1))
         ctx.enter_context(tc.manual_schedule())
 
         def load_channels_first(name, src):
@@ -65,8 +65,17 @@ def tile_spatialgcn_pb_kernel(tc, h, x1, adp, wg, bg, gamma, beta, rmean, rvar, 
         zeros = const.tile([P, 2 * P], BF16, name="zeros")
         nc.vector.memset(zeros[:], 0.0)
 
+        free_banks = list(range(8))
+
+        def take_bank():
+            index = free_banks[0]
+            free_banks.remove(index)
+            bank = psum.tile([P, BANK], F32, tag="bank%d" % index, name="bank%d" % index)
+            return index, bank
+
         def keep_warm(count):
-            bank = psum.tile([P, BANK], F32, tag="bank", name="warm_bank")
+            index, bank = take_bank()
+            free_banks.append(index)
             for i in range(count):
                 nc.tensor.matmul(bank[:, 0 : 2 * P], lhsT=zeros[:, 0:P], rhs=zeros[:], start=True, stop=True)
 
@@ -111,8 +120,22 @@ def tile_spatialgcn_pb_kernel(tc, h, x1, adp, wg, bg, gamma, beta, rmean, rvar, 
                 in_=operand["values"][:],
             )
 
+        def quantise_nodes(operand, nodes):
+            nc.vector.quantize_mx(
+                out=operand["codes"][:, nodes].bitcast(FP8X4),
+                scales=operand["scales"][:, nodes],
+                in_=operand["values"][:, nodes.start * PACK : nodes.stop * PACK],
+            )
+
+        def regroup_nodes(rows_tile, operand, nodes):
+            nc.vector.tensor_copy(
+                out=operand["values"][:, nodes.start * PACK : nodes.stop * PACK].rearrange("p (c i t) -> p c t i", i=4, t=PACK),
+                in_=rows_tile[:].rearrange("p (t n) -> p t n", t=PACK)[:, :, nodes].rearrange("p t (c i) -> p c t i", i=4),
+            )
+
         def transpose_256_rows(src_words, operand, first_col):
-            bank = psum.tile([P, BANK], F32, tag="bank", name="t_bank")
+            index, bank = take_bank()
+            free_banks.append(index)
             for u in range(2):
                 for r in range(2):
                     nc.tensor.transpose(
@@ -137,82 +160,82 @@ def tile_spatialgcn_pb_kernel(tc, h, x1, adp, wg, bg, gamma, beta, rmean, rvar, 
                 in_=rows_tile[:].rearrange("p (t c i) -> p c t i", t=PACK, i=4),
             )
 
-        def hop(b):
-            for j in range(TILES):
-                bank = psum.tile([P, BANK], F32, tag="bank", name="x2_bank")
-                for t in range(TILES):
-                    nc.tensor.matmul_mx(
-                        out=bank[:, t * P : (t + 1) * P],
-                        lhsT=x1T[b]["codes"][:, t * P : (t + 1) * P].bitcast(FP8X4),
-                        lhsT_scale=x1T[b]["scales"][:, t * P : (t + 1) * P],
-                        rhs=adpT["codes"][:, j * P : (j + 1) * P].bitcast(FP8X4),
-                        rhs_scale=adpT["scales"][:, j * P : (j + 1) * P],
-                        start=True,
-                        stop=True,
-                    )
-                nc.scalar.copy(
-                    out=cat[b][2]["values"][:, j * BANK : (j + 1) * BANK].rearrange("p (w t) -> p w t", t=PACK),
-                    in_=bank[:].rearrange("p (t w) -> p w t", t=PACK),
-                )
-
-        def conv(b):
-            def conv_pass(acc, ot, g, nodes):
-                unit = GROUPS * (ot % 2) + g
-                weights = wgT[ot // 2][unit // 2]
-                cols = slice((unit % 2) * P, (unit % 2 + 1) * P)
-                nc.tensor.matmul_mx(
-                    out=acc[:, 0 : nodes.stop - nodes.start],
-                    lhsT=weights["codes"][:, cols].bitcast(FP8X4),
-                    lhsT_scale=weights["scales"][:, cols],
-                    rhs=cat[b][g]["codes"][:, nodes].bitcast(FP8X4),
-                    rhs_scale=cat[b][g]["scales"][:, nodes],
-                    start=(g == CONV_ORDER[0]),
-                    stop=(g == CONV_ORDER[-1]),
-                )
-
-            def leave(acc, ot, nodes, on_scalar):
-                width = nodes.stop - nodes.start
-                result = results.tile([P, width], F32, name="result%d%d%d" % (b, ot, nodes.start))
-                if on_scalar:
-                    nc.scalar.activation(
-                        out=result[:],
-                        in_=acc[:, 0:width],
-                        func=ACT.Identity,
-                        scale=inv[:, ot : ot + 1],
-                        bias=shift[:, ot : ot + 1],
-                    )
-                else:
-                    nc.vector.tensor_scalar(
-                        out=result[:],
-                        in0=acc[:, 0:width],
-                        scalar1=inv[:, ot : ot + 1],
-                        scalar2=shift[:, ot : ot + 1],
-                        op0=ALU.mult,
-                        op1=ALU.add,
-                    )
-                nc.sync.dma_start(out=out_rows[:, ot, nodes], in_=result[:])
-
-            out_rows = out[b].rearrange("(p t) n -> p t n", t=TILES)
-            everything = slice(0, NODES)
-            if b == 0:
-                groups = [[(0, everything), (1, everything)], [(2, everything)], [(3, everything)]]
+        def copy_out(engine, out, in_):
+            if engine == "S":
+                nc.scalar.copy(out=out, in_=in_)
             else:
-                groups = [[(0, everything), (1, everything), (2, everything), (3, slice(0, 256)), (3, slice(256, 512))]]
-            for group in groups:
-                banks = []
-                for ot, nodes in group:
-                    acc = psum.tile([P, BANK], F32, tag="bank", name="acc")
-                    banks.append(acc)
-                    conv_pass(acc, ot, CONV_ORDER[0], nodes)
-                if b == 0:
-                    for g in CONV_ORDER[1:]:
-                        for acc, (ot, nodes) in zip(banks, group):
-                            conv_pass(acc, ot, g, nodes)
-                for acc, (ot, nodes) in zip(banks, group):
-                    if b == 1:
-                        for g in CONV_ORDER[1:]:
-                            conv_pass(acc, ot, g, nodes)
-                    leave(acc, ot, nodes, b == 0 or ot % 2 == 1 and nodes.start == 0)
+                nc.vector.tensor_copy(out=out, in_=in_)
+
+        def hop_product(b, j):
+            index, bank = take_bank()
+            for t in range(TILES):
+                nc.tensor.matmul_mx(
+                    out=bank[:, t * P : (t + 1) * P],
+                    lhsT=x1T[b]["codes"][:, t * P : (t + 1) * P].bitcast(FP8X4),
+                    lhsT_scale=x1T[b]["scales"][:, t * P : (t + 1) * P],
+                    rhs=adpT["codes"][:, j * P : (j + 1) * P].bitcast(FP8X4),
+                    rhs_scale=adpT["scales"][:, j * P : (j + 1) * P],
+                    start=True,
+                    stop=True,
+                )
+            return b, j, index, bank
+
+        def hop_out(product, engine="S"):
+            b, j, index, bank = product
+            free_banks.append(index)
+            copy_out(
+                engine,
+                out=cat[b][2]["values"][:, j * BANK : (j + 1) * BANK].rearrange("p (w t) -> p w t", t=PACK),
+                in_=bank[:].rearrange("p (t w) -> p w t", t=PACK),
+            )
+
+        everything = slice(0, NODES)
+
+        def conv_pass(tile_, g):
+            b, ot, nodes, acc, index = tile_
+            unit = GROUPS * (ot % 2) + g
+            weights = wgT[ot // 2][unit // 2]
+            cols = slice((unit % 2) * P, (unit % 2 + 1) * P)
+            nc.tensor.matmul_mx(
+                out=acc[:, 0 : nodes.stop - nodes.start],
+                lhsT=weights["codes"][:, cols].bitcast(FP8X4),
+                lhsT_scale=weights["scales"][:, cols],
+                rhs=cat[b][g]["codes"][:, nodes].bitcast(FP8X4),
+                rhs_scale=cat[b][g]["scales"][:, nodes],
+                start=(g == CONV_ORDER[b][0]),
+                stop=(g == CONV_ORDER[b][-1]),
+            )
+
+        def open_tile(b, ot, nodes=everything):
+            index, acc = take_bank()
+            tile_ = (b, ot, nodes, acc, index)
+            conv_pass(tile_, CONV_ORDER[b][0])
+            return tile_
+
+        def leave(tile_, engine):
+            b, ot, nodes, acc, index = tile_
+            free_banks.append(index)
+            width = nodes.stop - nodes.start
+            result = results.tile([P, width], F32, name="result%d%d%d" % (b, ot, nodes.start))
+            if engine == "S":
+                nc.scalar.activation(
+                    out=result[:],
+                    in_=acc[:, 0:width],
+                    func=ACT.Identity,
+                    scale=inv[:, ot : ot + 1],
+                    bias=shift[:, ot : ot + 1],
+                )
+            else:
+                nc.vector.tensor_scalar(
+                    out=result[:],
+                    in0=acc[:, 0:width],
+                    scalar1=inv[:, ot : ot + 1],
+                    scalar2=shift[:, ot : ot + 1],
+                    op0=ALU.mult,
+                    op1=ALU.add,
+                )
+            out_rows = out[b].rearrange("(p t) n -> p t n", t=TILES)
+            nc.sync.dma_start(out=out_rows[:, ot, nodes], in_=result[:])
 
         def transpose_wg_half(i):
             for m in range(GROUPS):
@@ -256,21 +279,47 @@ def tile_spatialgcn_pb_kernel(tc, h, x1, adp, wg, bg, gamma, beta, rmean, rvar, 
         quantise(cat[1][1])
         transpose_wg_half(0)
         quantise_wg_half(0)
-        hop(0)
-        transpose_wg_half(1)
+        products = [hop_product(0, j) for j in range(TILES)]
+        for j in range(3):
+            hop_out(products[j])
+        hop_out(products[3], "V")
         regroup(h_rows[0], cat[0][0])
+        transpose_wg_half(1)
+        first_pair = [open_tile(0, ot) for ot in range(2)]
         quantise(cat[0][2])
         quantise(cat[0][0])
-        quantise(wgT[1][0])
         nc.vector.tensor_mul(out=inv[:], in0=gamma_sb[:], in1=rstd[:])
         nc.vector.tensor_sub(out=centred[:], in0=bg_sb[:], in1=rmean_sb[:])
-        quantise(wgT[1][1])
+        quantise(wgT[1][0])
         nc.vector.tensor_mul(out=scaled[:], in0=centred[:], in1=inv[:])
-        quantise(wgT[1][2])
-        hop(1)
-        regroup(h_rows[1], cat[1][0])
+        quantise(wgT[1][1])
         nc.vector.tensor_add(out=shift[:], in0=scaled[:], in1=beta_sb[:])
+        quantise(wgT[1][2])
+        products = [hop_product(1, j) for j in range(TILES)]
+        batch1 = [open_tile(1, ot) for ot in range(2)]
+        hop_out(products[0])
+        hop_out(products[1])
+        hop_out(products[2])
+        for g in CONV_ORDER[0][1:]:
+            for tile_ in first_pair:
+                conv_pass(tile_, g)
+        leave(first_pair[0], "S")
+        hop_out(products[3])
+        leave(first_pair[1], "S")
+        for half in range(2):
+            regroup_nodes(h_rows[1], cat[1][0], slice(half * 256, half * 256 + 256))
+        for half in range(2):
+            quantise_nodes(cat[1][0], slice(half * 256, half * 256 + 256))
         quantise(cat[1][2])
-        quantise(cat[1][0])
-        conv(0)
-        conv(1)
+        for ot in range(2, TILES):
+            tile_ = open_tile(0, ot)
+            for g in CONV_ORDER[0][1:]:
+                conv_pass(tile_, g)
+            leave(tile_, "S")
+        batch1.append(open_tile(1, 2))
+        for half in range(2):
+            batch1.append(open_tile(1, 3, slice(half * 256, half * 256 + 256)))
+        for tile_, engine in zip(batch1, "VSVSV"):
+            for g in CONV_ORDER[1][1:]:
+                conv_pass(tile_, g)
+            leave(tile_, engine)

@@ -52,18 +52,21 @@ def tile_spatialgcn_pb_kernel(tc, h, x1, adp, wg, bg, gamma, beta, rmean, rvar, 
             return tile_
 
         def load_wg_half(i):
-            pieces = []
-            for m in range(GROUPS):
-                piece = rows.tile([P, PIECE], BF16, name="wg_rows%d%d" % (i, m))
-                first = (GROUPS * i + m) * PIECE
-                nc.sync.dma_start(out=piece[:], in_=wg_flat[:, first : first + PIECE])
-                pieces.append(piece)
-            return pieces
+            tile_ = rows.tile([P, GROUPS * PIECE], BF16, name="wg_rows%d" % i)
+            first = GROUPS * i * PIECE
+            edges = [0, 1, GROUPS] if i == 0 else [0, GROUPS]
+            for start, stop in zip(edges, edges[1:]):
+                nc.sync.dma_start(
+                    out=tile_[:, start * PIECE : stop * PIECE],
+                    in_=wg_flat[:, first + start * PIECE : first + stop * PIECE],
+                )
+            return tile_
 
         rvar_sb = load_channel_vector(nc.scalar, "rvar_sb", rvar)
 
-        zeros = const.tile([P, 2 * P], BF16, name="zeros")
-        nc.vector.memset(zeros[:], 0.0)
+        zeros = const.tile([P, BANK], BF16, name="zeros")
+        nc.vector.memset(zeros[:, 0 : 2 * P], 0.0)
+        nc.vector.memset(zeros[:, 2 * P : BANK], 0.0)
 
         free_banks = list(range(8))
 
@@ -73,11 +76,11 @@ def tile_spatialgcn_pb_kernel(tc, h, x1, adp, wg, bg, gamma, beta, rmean, rvar, 
             bank = psum.tile([P, BANK], F32, tag="bank%d" % index, name="bank%d" % index)
             return index, bank
 
-        def keep_warm(count):
+        def keep_warm(count, cols):
             index, bank = take_bank()
             free_banks.append(index)
             for i in range(count):
-                nc.tensor.matmul(bank[:, 0 : 2 * P], lhsT=zeros[:, 0:P], rhs=zeros[:], start=True, stop=True)
+                nc.tensor.matmul(bank[:, 0:cols], lhsT=zeros[:, 0:P], rhs=zeros[:, 0:cols], start=True, stop=True)
 
         x1_rows = [None, None]
         h_rows = [None, None]
@@ -87,17 +90,13 @@ def tile_spatialgcn_pb_kernel(tc, h, x1, adp, wg, bg, gamma, beta, rmean, rvar, 
                 out=x1_rows[0][:, u * 2 * NODES : (u + 1) * 2 * NODES],
                 in_=x1[0].rearrange("(u q e) n -> u q (e n)", u=2, e=2)[u],
             )
-        adp_rows = rows.tile([P, TILES * NODES], BF16, name="adp_rows")
-        nc.sync.dma_start(
-            out=adp_rows[:].rearrange("p (j v) -> p j v", j=TILES),
-            in_=adp.rearrange("(j p) v -> p j v", p=P),
-        )
+        adp_rows = load_channels_first("adp_rows", adp)
         x1_rows[1] = load_channels_first("x1_rows1", x1[1])
         wg_flat = wg.rearrange("(p t) c -> p (t c)", t=TILES)
         wg_rows = [None, None]
         wg_rows[0] = load_wg_half(0)
-        h_rows[0] = load_channels_first("h_rows0", h[0])
         wg_rows[1] = load_wg_half(1)
+        h_rows[0] = load_channels_first("h_rows0", h[0])
         h_rows[1] = load_channels_first("h_rows1", h[1])
         gamma_sb = load_channel_vector(nc.sync, "gamma_sb", gamma)
         bg_sb = load_channel_vector(nc.sync, "bg_sb", bg)
@@ -133,7 +132,7 @@ def tile_spatialgcn_pb_kernel(tc, h, x1, adp, wg, bg, gamma, beta, rmean, rvar, 
                 in_=rows_tile[:].rearrange("p (t n) -> p t n", t=PACK)[:, :, nodes].rearrange("p t (c i) -> p c t i", i=4),
             )
 
-        def transpose_256_rows(src_words, operand, first_col):
+        def transpose_256_rows(src_words, operand, first_col, in_order=False):
             index, bank = take_bank()
             free_banks.append(index)
             for u in range(2):
@@ -144,15 +143,22 @@ def tile_spatialgcn_pb_kernel(tc, h, x1, adp, wg, bg, gamma, beta, rmean, rvar, 
                         ident[:],
                     )
             words = operand["values"][:].bitcast(F32)
-            nc.scalar.copy(
-                out=words[:, 2 * first_col : 2 * first_col + BANK].rearrange("p (c u) -> p c u", u=2),
-                in_=bank[:].rearrange("p (u c) -> p c u", u=2),
-            )
+            out_words = words[:, 2 * first_col : 2 * first_col + BANK]
+            if in_order:
+                nc.scalar.copy(
+                    out=out_words.rearrange("p (c r u) -> p c r u", r=2, u=2),
+                    in_=bank[:].rearrange("p (u r c) -> p c r u", r=2, u=2),
+                )
+            else:
+                nc.scalar.copy(
+                    out=out_words.rearrange("p (c u) -> p c u", u=2),
+                    in_=bank[:].rearrange("p (u c) -> p c u", u=2),
+                )
 
-        def transpose_512_rows(rows_tile, operand):
+        def transpose_512_rows(rows_tile, operand, in_order=False):
             src_words = rows_tile[:].bitcast(F32).rearrange("p (t m) -> p t m", t=TILES)
             for i in range(2):
-                transpose_256_rows(src_words[:, 2 * i : 2 * i + 2, :], operand, 256 * i)
+                transpose_256_rows(src_words[:, 2 * i : 2 * i + 2, :], operand, 256 * i, in_order)
 
         def regroup(rows_tile, operand):
             nc.vector.tensor_copy(
@@ -239,7 +245,7 @@ def tile_spatialgcn_pb_kernel(tc, h, x1, adp, wg, bg, gamma, beta, rmean, rvar, 
 
         def transpose_wg_half(i):
             for m in range(GROUPS):
-                unit_words = wg_rows[i][m][:].bitcast(F32).rearrange("p (k w) -> p k w", k=2)
+                unit_words = wg_rows[i][:, m * PIECE : (m + 1) * PIECE].bitcast(F32).rearrange("p (k w) -> p k w", k=2)
                 transpose_256_rows(unit_words, wgT[i][m], 0)
 
         def quantise_wg_half(i):
@@ -261,20 +267,20 @@ def tile_spatialgcn_pb_kernel(tc, h, x1, adp, wg, bg, gamma, beta, rmean, rvar, 
         nc.vector.tensor_scalar_add(out=var_eps[:], in0=rvar_sb[:], scalar1=EPS)
         nc.scalar.sqrt(out=std[:], in_=var_eps[:])
 
-        keep_warm(8)
+        keep_warm(8, 2 * P)
         regroup(x1_rows[0], cat[0][1])
         transpose_512_rows(x1_rows[0], x1T[0])
-        keep_warm(4)
+        keep_warm(2, BANK)
 
         nc.vector.reciprocal(out=rstd[:], in_=std[:])
         quantise(cat[0][1])
         quantise(x1T[0])
-        transpose_512_rows(adp_rows, adpT)
-        keep_warm(4)
+        transpose_512_rows(adp_rows, adpT, in_order=True)
+        keep_warm(2, BANK)
         regroup(x1_rows[1], cat[1][1])
         quantise(adpT)
         transpose_512_rows(x1_rows[1], x1T[1])
-        keep_warm(4)
+        keep_warm(2, BANK)
         quantise(x1T[1])
         quantise(cat[1][1])
         transpose_wg_half(0)

@@ -97,11 +97,11 @@ def tile_spatialgcn_pb_kernel(tc, h, x1, adp, wg, bg, gamma, beta, rmean, rvar, 
         wg_rows[0] = load_wg_half(0)
         wg_rows[1] = load_wg_half(1)
         h_rows[0] = load_channels_first("h_rows0", h[0])
-        h_rows[1] = load_channels_first("h_rows1", h[1])
         gamma_sb = load_channel_vector(nc.sync, "gamma_sb", gamma)
         bg_sb = load_channel_vector(nc.sync, "bg_sb", bg)
         rmean_sb = load_channel_vector(nc.sync, "rmean_sb", rmean)
         beta_sb = load_channel_vector(nc.sync, "beta_sb", beta)
+        h_rows[1] = load_channels_first("h_rows1", h[1])
 
         ident = const.tile([P, P], F32, name="ident")
         make_identity(nc, ident[:])
@@ -268,12 +268,14 @@ def tile_spatialgcn_pb_kernel(tc, h, x1, adp, wg, bg, gamma, beta, rmean, rvar, 
         nc.scalar.sqrt(out=std[:], in_=var_eps[:])
 
         keep_warm(8, 2 * P)
-        regroup(x1_rows[0], cat[0][1])
+        for half in range(2):
+            regroup_nodes(x1_rows[0], cat[0][1], slice(half * 256, half * 256 + 256))
         transpose_512_rows(x1_rows[0], x1T[0])
         keep_warm(2, BANK)
 
         nc.vector.reciprocal(out=rstd[:], in_=std[:])
-        quantise(cat[0][1])
+        for half in range(2):
+            quantise_nodes(cat[0][1], slice(half * 256, half * 256 + 256))
         quantise(x1T[0])
         transpose_512_rows(adp_rows, adpT, in_order=True)
         keep_warm(2, BANK)

from contextlib import ExitStack

import concourse.mybir as mybir
from concourse.masks import make_identity

F32 = mybir.dt.float32
BF16 = mybir.dt.bfloat16
U32 = mybir.dt.uint32
U8 = mybir.dt.uint8
FP8X4 = mybir.dt.float8_e4m3fn_x4
ACT = mybir.ActivationFunctionType
ALU = mybir.AluOpType

P = 128
PACK = 4
K_PASS = P * PACK
BATCH = 2
CH = 512
NODES = 512
GROUPS = 3
TILES = 4
BANK = 512
PIECE = 2 * BANK
EPS = 1e-5
CONV_ORDER = ((1, 2, 0), (1, 0, 2))

FLOPS = 2 * BATCH * CH * NODES * NODES + 2 * BATCH * CH * GROUPS * CH * NODES


def tile_spatialgcn_pb_kernel(tc, h, x1, adp, wg, bg, gamma, beta, rmean, rvar, out):
    nc = tc.nc
    with ExitStack() as ctx:
        const = ctx.enter_context(tc.tile_pool(name="const", bufs=1))
        rows = ctx.enter_context(tc.tile_pool(name="rows", bufs=1))
        grouped = ctx.enter_context(tc.tile_pool(name="grouped", bufs=1))
        mx = ctx.enter_context(tc.tile_pool(name="mx", bufs=1))
        results = ctx.enter_context(tc.tile_pool(name="results", bufs=1))
        psum = ctx.enter_context(tc.psum_pool(name="psum", bufs=1))
        ctx.enter_context(tc.manual_schedule())

        def load_channels_first(name, src):
            tile_ = rows.tile([P, PACK * NODES], BF16, name=name)
            nc.sync.dma_start(
                out=tile_[:].rearrange("p (u r) -> p u r", u=2),
                in_=src.rearrange("(u q e) n -> q u (e n)", u=2, e=2),
            )
            return tile_

        def load_channel_vector(queue, name, vec):
            tile_ = const.tile([P, TILES], BF16, name=name)
            queue.dma_start(out=tile_[:], in_=vec.rearrange("(p t) -> p t", t=TILES))
            return tile_

        def load_wg_half(i):
            tile_ = rows.tile([P, GROUPS * PIECE], BF16, name="wg_rows%d" % i)
            first = GROUPS * i * PIECE
            edges = [0, 1, GROUPS] if i == 0 else [0, GROUPS]
            for start, stop in zip(edges, edges[1:]):
                nc.sync.dma_start(
                    out=tile_[:, start * PIECE : stop * PIECE],
                    in_=wg_flat[:, first + start * PIECE : first + stop * PIECE],
                )
            return tile_

        rvar_sb = load_channel_vector(nc.scalar, "rvar_sb", rvar)

        zeros = const.tile([P, BANK], BF16, name="zeros")
        nc.vector.memset(zeros[:, 0 : 2 * P], 0.0)
        nc.vector.memset(zeros[:, 2 * P : BANK], 0.0)

        free_banks = list(range(8))

        def take_bank():
            index = free_banks[0]
            free_banks.remove(index)
            bank = psum.tile([P, BANK], F32, tag="bank%d" % index, name="bank%d" % index)
            return index, bank

        def keep_warm(count, cols):
            index, bank = take_bank()
            free_banks.append(index)
            for i in range(count):
                nc.tensor.matmul(bank[:, 0:cols], lhsT=zeros[:, 0:P], rhs=zeros[:, 0:cols], start=True, stop=True)

        x1_rows = [None, None]
        h_rows = [None, None]
        x1_rows[0] = rows.tile([P, PACK * NODES], BF16, name="x1_rows0")
        for u in range(2):
            nc.sync.dma_start(
                out=x1_rows[0][:, u * 2 * NODES : (u + 1) * 2 * NODES],
                in_=x1[0].rearrange("(u q e) n -> u q (e n)", u=2, e=2)[u],
            )
        adp_rows = load_channels_first("adp_rows", adp)
        x1_rows[1] = load_channels_first("x1_rows1", x1[1])
        wg_flat = wg.rearrange("(p t) c -> p (t c)", t=TILES)
        wg_rows = [None, None]
        wg_rows[0] = load_wg_half(0)
        wg_rows[1] = load_wg_half(1)
        h_rows[0] = load_channels_first("h_rows0", h[0])
        gamma_sb = load_channel_vector(nc.sync, "gamma_sb", gamma)
        bg_sb = load_channel_vector(nc.sync, "bg_sb", bg)
        rmean_sb = load_channel_vector(nc.sync, "rmean_sb", rmean)
        beta_sb = load_channel_vector(nc.sync, "beta_sb", beta)
        h_rows[1] = load_channels_first("h_rows1", h[1])

        ident = const.tile([P, P], F32, name="ident")
        make_identity(nc, ident[:])

        def new_operand(name, cols):
            values = grouped.tile([P, cols * PACK], BF16, name=name + "_values", align_bytes=64)
            codes = mx.tile([P, cols], U32, name=name + "_codes", align_bytes=64)
            scales = mx.tile([P, cols], U8, name=name + "_scales", align_bytes=64)
            return {"values": values, "codes": codes, "scales": scales}

        def quantise(operand):
            nc.vector.quantize_mx(
                out=operand["codes"][:].bitcast(FP8X4),
                scales=operand["scales"][:],
                in_=operand["values"][:],
            )

        def quantise_nodes(operand, nodes):
            nc.vector.quantize_mx(
                out=operand["codes"][:, nodes].bitcast(FP8X4),
                scales=operand["scales"][:, nodes],
                in_=operand["values"][:, nodes.start * PACK : nodes.stop * PACK],
            )

        def regroup_nodes(rows_tile, operand, nodes):
            nc.vector.tensor_copy(
                out=operand["values"][:, nodes.start * PACK : nodes.stop * PACK].rearrange("p (c i t) -> p c t i", i=4, t=PACK),
                in_=rows_tile[:].rearrange("p (t n) -> p t n", t=PACK)[:, :, nodes].rearrange("p t (c i) -> p c t i", i=4),
            )

        def transpose_256_rows(src_words, operand, first_col, in_order=False):
            index, bank = take_bank()
            free_banks.append(index)
            for u in range(2):
                for r in range(2):
                    nc.tensor.transpose(
                        bank[:, (2 * u + r) * P : (2 * u + r + 1) * P],
                        src_words[:, r, u * P : (u + 1) * P],
                        ident[:],
                    )
            words = operand["values"][:].bitcast(F32)
            out_words = words[:, 2 * first_col : 2 * first_col + BANK]
            if in_order:
                nc.scalar.copy(
                    out=out_words.rearrange("p (c r u) -> p c r u", r=2, u=2),
                    in_=bank[:].rearrange("p (u r c) -> p c r u", r=2, u=2),
                )
            else:
                nc.scalar.copy(
                    out=out_words.rearrange("p (c u) -> p c u", u=2),
                    in_=bank[:].rearrange("p (u c) -> p c u", u=2),
                )

        def transpose_512_rows(rows_tile, operand, in_order=False):
            src_words = rows_tile[:].bitcast(F32).rearrange("p (t m) -> p t m", t=TILES)
            for i in range(2):
                transpose_256_rows(src_words[:, 2 * i : 2 * i + 2, :], operand, 256 * i, in_order)

        def regroup(rows_tile, operand):
            nc.vector.tensor_copy(
                out=operand["values"][:].rearrange("p (c i t) -> p c t i", i=4, t=PACK),
                in_=rows_tile[:].rearrange("p (t c i) -> p c t i", t=PACK, i=4),
            )

        def copy_out(engine, out, in_):
            if engine == "S":
                nc.scalar.copy(out=out, in_=in_)
            else:
                nc.vector.tensor_copy(out=out, in_=in_)

        def hop_product(b, j):
            index, bank = take_bank()
            for t in range(TILES):
                nc.tensor.matmul_mx(
                    out=bank[:, t * P : (t + 1) * P],
                    lhsT=x1T[b]["codes"][:, t * P : (t + 1) * P].bitcast(FP8X4),
                    lhsT_scale=x1T[b]["scales"][:, t * P : (t + 1) * P],
                    rhs=adpT["codes"][:, j * P : (j + 1) * P].bitcast(FP8X4),
                    rhs_scale=adpT["scales"][:, j * P : (j + 1) * P],
                    start=True,
                    stop=True,
                )
            return b, j, index, bank

        def hop_out(product, engine="S"):
            b, j, index, bank = product
            free_banks.append(index)
            copy_out(
                engine,
                out=cat[b][2]["values"][:, j * BANK : (j + 1) * BANK].rearrange("p (w t) -> p w t", t=PACK),
                in_=bank[:].rearrange("p (t w) -> p w t", t=PACK),
            )

        everything = slice(0, NODES)

        def conv_pass(tile_, g):
            b, ot, nodes, acc, index = tile_
            unit = GROUPS * (ot % 2) + g
            weights = wgT[ot // 2][unit // 2]
            cols = slice((unit % 2) * P, (unit % 2 + 1) * P)
            nc.tensor.matmul_mx(
                out=acc[:, 0 : nodes.stop - nodes.start],
                lhsT=weights["codes"][:, cols].bitcast(FP8X4),
                lhsT_scale=weights["scales"][:, cols],
                rhs=cat[b][g]["codes"][:, nodes].bitcast(FP8X4),
                rhs_scale=cat[b][g]["scales"][:, nodes],
                start=(g == CONV_ORDER[b][0]),
                stop=(g == CONV_ORDER[b][-1]),
            )

        def open_tile(b, ot, nodes=everything):
            index, acc = take_bank()
            tile_ = (b, ot, nodes, acc, index)
            conv_pass(tile_, CONV_ORDER[b][0])
            return tile_

        def leave(tile_, engine):
            b, ot, nodes, acc, index = tile_
            free_banks.append(index)
            width = nodes.stop - nodes.start
            result = results.tile([P, width], F32, name="result%d%d%d" % (b, ot, nodes.start))
            if engine == "S":
                nc.scalar.activation(
                    out=result[:],
                    in_=acc[:, 0:width],
                    func=ACT.Identity,
                    scale=inv[:, ot : ot + 1],
                    bias=shift[:, ot : ot + 1],
                )
            else:
                nc.vector.tensor_scalar(
                    out=result[:],
                    in0=acc[:, 0:width],
                    scalar1=inv[:, ot : ot + 1],
                    scalar2=shift[:, ot : ot + 1],
                    op0=ALU.mult,
                    op1=ALU.add,
                )
            out_rows = out[b].rearrange("(p t) n -> p t n", t=TILES)
            nc.sync.dma_start(out=out_rows[:, ot, nodes], in_=result[:])

        def transpose_wg_half(i):
            for m in range(GROUPS):
                unit_words = wg_rows[i][:, m * PIECE : (m + 1) * PIECE].bitcast(F32).rearrange("p (k w) -> p k w", k=2)
                transpose_256_rows(unit_words, wgT[i][m], 0)

        def quantise_wg_half(i):
            for m in range(GROUPS):
                quantise(wgT[i][m])

        x1T = [new_operand("x1T%d" % b, CH) for b in range(BATCH)]
        adpT = new_operand("adpT", NODES)
        wgT = [[new_operand("wgT%d%d" % (i, m), 2 * P) for m in range(GROUPS)] for i in range(2)]
        cat = [[new_operand("cat%d%d" % (b, g), NODES) for g in range(GROUPS)] for b in range(BATCH)]

        var_eps = const.tile([P, TILES], F32, name="var_eps")
        std = const.tile([P, TILES], F32, name="std")
        rstd = const.tile([P, TILES], F32, name="rstd")
        inv = const.tile([P, TILES], F32, name="inv")
        centred = const.tile([P, TILES], F32, name="centred")
        scaled = const.tile([P, TILES], F32, name="scaled")
        shift = const.tile([P, TILES], F32, name="shift")
        nc.vector.tensor_scalar_add(out=var_eps[:], in0=rvar_sb[:], scalar1=EPS)
        nc.scalar.sqrt(out=std[:], in_=var_eps[:])

        keep_warm(8, 2 * P)
        for half in range(2):
            regroup_nodes(x1_rows[0], cat[0][1], slice(half * 256, half * 256 + 256))
        transpose_512_rows(x1_rows[0], x1T[0])
        keep_warm(2, BANK)

        nc.vector.reciprocal(out=rstd[:], in_=std[:])
        for half in range(2):
            quantise_nodes(cat[0][1], slice(half * 256, half * 256 + 256))
        quantise(x1T[0])
        transpose_512_rows(adp_rows, adpT, in_order=True)
        keep_warm(2, BANK)
        regroup(x1_rows[1], cat[1][1])
        quantise(adpT)
        transpose_512_rows(x1_rows[1], x1T[1])
        keep_warm(2, BANK)
        quantise(x1T[1])
        quantise(cat[1][1])
        transpose_wg_half(0)
        quantise_wg_half(0)
        products = [hop_product(0, j) for j in range(TILES)]
        for j in range(3):
            hop_out(products[j])
        hop_out(products[3], "V")
        regroup(h_rows[0], cat[0][0])
        transpose_wg_half(1)
        first_pair = [open_tile(0, ot) for ot in range(2)]
        quantise(cat[0][2])
        quantise(cat[0][0])
        nc.vector.tensor_mul(out=inv[:], in0=gamma_sb[:], in1=rstd[:])
        nc.vector.tensor_sub(out=centred[:], in0=bg_sb[:], in1=rmean_sb[:])
        quantise(wgT[1][0])
        nc.vector.tensor_mul(out=scaled[:], in0=centred[:], in1=inv[:])
        quantise(wgT[1][1])
        nc.vector.tensor_add(out=shift[:], in0=scaled[:], in1=beta_sb[:])
        quantise(wgT[1][2])
        products = [hop_product(1, j) for j in range(TILES)]
        batch1 = [open_tile(1, ot) for ot in range(2)]
        hop_out(products[0])
        hop_out(products[1])
        hop_out(products[2])
        for g in CONV_ORDER[0][1:]:
            for tile_ in first_pair:
                conv_pass(tile_, g)
        leave(first_pair[0], "S")
        hop_out(products[3])
        leave(first_pair[1], "S")
        for half in range(2):
            regroup_nodes(h_rows[1], cat[1][0], slice(half * 256, half * 256 + 256))
        for half in range(2):
            quantise_nodes(cat[1][0], slice(half * 256, half * 256 + 256))
        quantise(cat[1][2])
        for ot in range(2, TILES):
            tile_ = open_tile(0, ot)
            for g in CONV_ORDER[0][1:]:
                conv_pass(tile_, g)
            leave(tile_, "S")
        batch1.append(open_tile(1, 2))
        for half in range(2):
            batch1.append(open_tile(1, 3, slice(half * 256, half * 256 + 256)))
        for tile_, engine in zip(batch1, "VSVSV"):
            for g in CONV_ORDER[1][1:]:
                conv_pass(tile_, g)
            leave(tile_, engine)
